import numpy as np
import ml_dtypes


def mxq(x, axis, fmt="e4m3"):
    dtype, down = {"e4m3": (ml_dtypes.float8_e4m3fn, 7), "e5m2": (ml_dtypes.float8_e5m2, 14)}[fmt]
    v = np.moveaxis(np.asarray(x, np.float32).astype(ml_dtypes.bfloat16).astype(np.float64), axis, -1)
    blocks = v.reshape(v.shape[:-1] + (-1, 32))
    amax = np.abs(blocks).max(-1, keepdims=True)
    byte = np.maximum(np.where(amax > 0, np.frexp(amax)[1] - 1 + 127, 0) - down, 1)
    scale = np.exp2(byte - 127.0)
    codes = (blocks / scale).astype(np.float32).astype(dtype).astype(np.float64)
    return np.moveaxis((codes * scale).reshape(v.shape), -1, axis)


WIDE = False


def mx_kscale(k):
    if not WIDE:
        return np.ones(k)
    levels = np.array([10, -10, 5, -5, 0])
    if k % 512:
        return np.exp2(np.random.permutation(np.resize(levels, k // 32))).repeat(32)
    a = np.empty((k // 512, 16))
    for p in range(k // 512):
        a[p, :8] = np.random.permutation(np.resize(levels, 8))
        for g in range(8):
            far = levels[np.abs(levels - a[p, g]) >= 10]
            a[p, g + 8] = far[np.random.randint(len(far))]
    return np.exp2(a.ravel()).repeat(32)


BF16 = ml_dtypes.bfloat16


def bf(x):
    return np.asarray(x, np.float32).astype(BF16)


def f64(x):
    return np.asarray(x).astype(np.float64)


B, S, D1, D2, DK, OUT = 1, 1024, 512, 512, 512, 512
EPS = 1e-5


def relu(x):
    return np.maximum(x, 0.0)


def layernorm(x, gamma, beta):
    mu = x.mean(-1, keepdims=True)
    var = np.square(x - mu).mean(-1, keepdims=True)
    return (x - mu) / np.sqrt(var + EPS) * gamma + beta


def draw0():
    r = np.random.standard_normal
    s, t = mx_kscale(DK), mx_kscale(OUT)
    return {"q": bf(r((B, S, DK)) * 0.55 * s), "q_hat": bf(r((B, S, DK)) * 0.3 * s),
            "W0": bf(r((OUT, DK)) / np.sqrt(DK) / s), "b0": bf(r(OUT) * 0.2),
            "W1": bf(r((OUT, DK)) / np.sqrt(DK) / s), "b1": bf(r(OUT) * 0.2),
            "W2": bf(r((OUT, DK)) / np.sqrt(DK) / s), "b2": bf(r(OUT) * 0.2),
            "W3": bf(r((OUT, DK)) / np.sqrt(DK) / s), "b3": bf(r(OUT) * 0.2),
            "gG": bf((1.0 + 0.1 * r(OUT)) * t), "betaG": bf(0.2 * r(OUT) * t),
            "gE": bf(1.0 + 0.1 * r(OUT)), "betaE": bf(0.2 * r(OUT)),
            "Wc": bf(r((OUT, OUT)) / np.sqrt(OUT) / t), "bc": bf(r(OUT) * 0.2)}


def core(q, q_hat, W0, b0, W1, b1, W2, b2, W3, b3, gG, betaG, gE, betaE, Wc, bc):
    qq = mxq(f64(q), 2, "e4m3")
    hq = mxq(f64(q_hat), 2, "e4m3")
    a0 = (qq @ mxq(f64(W0).T, 0, "e4m3")) + f64(b0)
    a1 = (hq @ mxq(f64(W1).T, 0, "e4m3")) + f64(b1)
    a2 = (hq @ mxq(f64(W2).T, 0, "e4m3")) + f64(b2)
    a3 = (qq @ mxq(f64(W3).T, 0, "e4m3")) + f64(b3)
    g = layernorm(relu(relu(a0) + relu(a1)), f64(gG), f64(betaG))
    e = layernorm(relu(relu(a2)), f64(gE), f64(betaE))
    c = relu((mxq(g * e, 2, "e4m3") @ mxq(f64(Wc).T, 0, "e4m3")) + f64(bc))
    q_out = relu(a3)
    return q_out + c


def e4m3fn_bytes(y):
    return np.clip(np.asarray(y, np.float64), -448.0, 448.0).astype(np.float32).astype(ml_dtypes.float8_e4m3fn).view(np.uint8)


def e4m3fn_values(b):
    return np.asarray(b, np.uint8).view(ml_dtypes.float8_e4m3fn).astype(np.float64)


def setup_inputs():
    d = draw0()
    x0 = np.asarray(d['q_hat']).astype(np.float64)
    s = (np.max(np.abs(x0), axis=(0, 1), keepdims=True) / 448.0).astype(np.float32)
    out = {}
    for k, v in d.items():
        if k == 'q_hat':
            out['q_hat_bytes'] = e4m3fn_bytes(x0 / s.astype(np.float64))
            out['q_hat_scale'] = s
        else:
            out[k] = v
    return out


def reference(q, q_hat_bytes, q_hat_scale, W0, b0, W1, b1, W2, b2, W3, b3, gG, betaG, gE, betaE, Wc, bc):
    return core(q, e4m3fn_values(q_hat_bytes) * q_hat_scale.astype(np.float64), W0, b0, W1, b1, W2, b2, W3, b3, gG, betaG, gE, betaE, Wc, bc)

from contextlib import ExitStack

import concourse.mybir as mybir
from concourse.masks import make_identity

S, D = 1024, 512
FLOPS = 5 * 2 * S * D * D
EPS = 1e-5

F32 = mybir.dt.float32
BF16 = mybir.dt.bfloat16
U32 = mybir.dt.uint32
U8 = mybir.dt.uint8
FP8 = mybir.dt.float8_e4m3fn
FP8X4 = mybir.dt.float8_e4m3fn_x4
ALU = mybir.AluOpType
ACT = mybir.ActivationFunctionType

P = 128
T = 4
HALVES = 2
GN = 256

ORDER = """
scT:m:2 scC.V uT.w0.1:s:3 uT.w0.0:s:0 uC.w0.1.S uC.w0.0.S uT.q0.1:m:2 prod.0.1 uT.q0.0:m:0 uT.w1.1:m:1
prod.0.0 uT.w1.0:s:1 uC.q0.0.S uC.w1.1.S uQ.w0 uC.w1.0.S uC.q0.1.V prod.0.2 uQ.q0.0 uT.x0.0:s:0 uQ.q0.1
uT.w2.0:m:0 prod.0.3 uT.w2.1:s:2 uT.x0.1:m:0 uC.x0.0.S uQ.w1 prod.1.1 bbT:s:0 uC.w2.0.S uC.w2.1.S prod.1.0
aM.0.0.0:m:0 uC.x0.1.S aM.1.1.0:m:0 aM.0.1.0:m:0 prod.1.2 uT.w3.1:s:0 uQ.x0.0 uT.x1.0:s:0 aR.0.2.S uQ.w2
aR.0.1.V aM.0.1.1:m:0 bbC.S aM.0.1.2:s:0 aR.0.0.V aM.0.0.1:s:0 aR.1.3.V aR.0.3.V uC.w3.1.S uQ.x0.1 prod.1.3
aS.0.3 uT.w3.0:s:0 uC.x1.0.S aY.0.3.S aR.1.2.V uT.q1.1:m:0 aY.0.2.S aM.1.1.1:s:0 aM.0.0.2:s:0 uT.q1.0:m:0
aS.0.1 uC.w3.0.S aS.0.2 uC.q1.1.S aS.0.0 aM.1.0.0:m:0 aS.1.3 aS.1.2 aY.0.0.S aY.0.1.S uQ.w3 aM.1.1.2:m:0
uQ.x1.0 aM.1.0.2:s:0 bT.0.0:m:0 uC.q1.0.S uQ.q1.1 uQ.q1.0 bT.0.1:m:0 uT.x1.1:s:0 aR.1.0.S aR.1.1.V
aM.1.0.1:s:0 aY.1.1.S aY.1.3.S aM.2.0.0:s:0 aY.1.0.S bS.0.0 bS.0.1 aY.1.2.S aM.3.1.0:s:0 bT.1.0:m:0 uC.x1.1.S
aS.1.1 bT.1.1:m:0 uT.wc.0:s:0 aR.2.0.V aS.1.0 uQ.x1.1 bA.0 aR.2.1.S aR.3.3.S bQ.0 bS.1.0 bS.1.1 eM.7:s:0 bR.0
eM.4:s:0 aR.3.2.S eM.5:s:0 uC.wc.0.S bN.0.0.S eU.7 bA.1 bQ.1 bN.0.1.S eU.5 bR.1 bT.2.0:s:0 bT.2.1:s:0 bN.1.0.S
uT.wc.1:m:0 eU.4 bS.2.0 bS.2.1 uC.wc.1.S aM.2.0.1:m:1 bT.3.0:s:0 aS.2.0 bA.2 aS.2.1 cT.0.0.0:m:0 bS.3.0
bN.1.1.S bT.3.1:s:0 eM.6:m:0 bQ.2 aM.2.1.0:m:0 cT.0.1.1:m:0 cE.0.1.0.S cE.0.0.0.S eY.7.G eY.4.G bR.2 eY.5.G
bS.3.1 aR.2.3.V bA.3 bN.2.0.S bN.2.1.S eU.6 bQ.3 aM.2.1.1:s:0 bR.3 rM.1.1:s:0 aR.2.2.S cE.0.2.1.S bN.3.0.S
aM.3.1.1:m:0 bS.7.1 bN.3.1.S aM.3.0.0:m:1 rM.0.1:s:0 aS.2.3 rM.0.3:m:0 bS.5.1 eY.6.G cT.0.0.1:s:0 aR.3.1.S
r3S.1.1.V aS.2.2 cE.0.3.1.S aS.3.2 r3S.0.3.S bT.4.0:s:0 bT.5.0:s:0 r3S.0.1.S aS.3.3 bS.4.1 aR.3.0.V bS.5.0
bS.4.0 cE.0.1.1.S rM.1.3:m:0 aM.3.0.1:m:0 cT.1.0.0:s:0 cE.0.0.1.S cT.0.1.0:m:0 bA.5 r3S.1.3.S cE.1.0.0.S
aS.3.1 bQ.5 cE.0.2.0.S bA.4 aS.3.0 cT.1.1.0:m:0 bS.6.1 cE.0.3.0.S cT.1.0.1:m:0 cE.1.2.0.V cE.1.3.0.S
cT.1.1.1:s:0 bR.5 bN.5.1.V bQ.4 bT.6.0:m:0 bN.4.1.V cE.1.0.1.S bR.4 bT.7.0:m:0 cE.1.3.1.S bS.6.0 bS.7.0 bA.6
cM.0.0.V bN.4.0.S rM.0.2:m:0 bN.5.0.S cE.1.1.1.S cM.0.1.G bQ.6 rM.0.0:s:1 bA.7 cE.1.2.1.S uQ.wc cE.1.1.0.S
bR.6 cQ.0 cM.1.1.V cM.1.0.V cT.2.1.0:m:0 bQ.7 bN.6.0.S bR.7 bN.7.0.S rM.1.0:s:0 cT.2.0.1:s:0 bN.6.1.G bN.7.1.G
cT.2.0.0:s:1 r3S.0.2.S r3S.0.0.V cT.2.1.1:m:0 cE.2.0.1.S cE.2.3.0.S r3S.1.0.V cE.2.1.1.S cE.2.2.0.V cE.2.3.1.V
cE.2.2.1.S cT.3.0.0:m:0 dM.0.0:s:0 cE.2.0.0.V dM.0.1:m:0 dS.0.0 cE.2.1.0.S cQ.1 cE.3.0.0.S dS.0.2 cT.3.0.1:m:0
cM.2.0.V cT.3.1.0:s:0 dS.0.1 cE.3.1.0.S cE.3.0.1.S dS.0.3 cM.2.1.G cT.3.1.1:s:0 rM.1.2:s:0 dM.1.1:m:0 cQ.2
dS.1.3 cE.3.3.0.S dM.1.0:m:0 dS.1.1 dS.1.0 dT.0.0:s:0 cE.3.2.0.S dS.1.2 dT.0.1:s:0 dM.2.0:m:0 cE.3.1.1.S
cE.3.2.1.S cE.3.3.1.S cM.3.1.V dS.2.0 dT.1.1:m:1 cM.3.0.G cQ.3 dT.1.0:m:0 dS.2.1 dM.2.1:s:0 r3S.1.2.S dC.0.0.S
dM.3.0:m:0 dC.0.1.S dS.2.3 dS.2.2 dS.3.0 dS.3.1 dM.3.1:m:0 dC.1.1.S dS.3.2 dT.2.1:m:0 dS.3.3 dC.1.0.S
dT.2.0:m:0 dT.3.0:s:0 dC.2.1.S dC.2.0.V dT.3.1:s:0 dC.3.0.V dC.3.1.S
"""


def tile_pregatingcontextualattentiongate_pb_kernel(
    tc, q, q_hat_bytes, q_hat_scale, W0, b0, W1, b1, W2, b2, W3, b3, gG, betaG, gE, betaE, Wc, bc, out
):
    nc = tc.nc
    with ExitStack() as ctx:
        const = ctx.enter_context(tc.tile_pool(name="const", bufs=1))
        raw = ctx.enter_context(tc.tile_pool(name="raw", bufs=1))
        work = ctx.enter_context(tc.tile_pool(name="work", bufs=2))
        psm = ctx.enter_context(tc.psum_pool(name="psm", bufs=4))
        pss = ctx.enter_context(tc.psum_pool(name="pss", bufs=4))
        pools = {"m": psm, "s": pss}

        ctx.enter_context(tc.manual_schedule())

        scale_cols = const.tile([P, T], F32, name="scale_cols")
        nc.scalar.dma_start(out=scale_cols[:], in_=q_hat_scale[0, 0].rearrange("(p t) -> p t", t=T))
        zeros = const.tile([P, 512], BF16, name="zeros")
        nc.vector.memset(zeros[:], 0.0)
        warm = const.tile([P, 1], F32, name="warm")
        nc.vector.memset(warm[:], 1.0)
        nc.scalar.activation(out=warm[:], in_=warm[:], func=ACT.Abs_reciprocal_sqrt)
        vec_bf = const.tile([P, 9, 16], BF16, name="vec_bf")

        ident = const.tile([P, P], F32, name="ident")
        make_identity(nc, ident[:])

        w_view = "(m t) k -> m t k"
        q_view = q[0].rearrange("(h p j) k -> h p j k", h=HALVES, j=T)
        qh_view = q_hat_bytes[0].rearrange("(h p j) k -> h p j k", h=HALVES, j=T)
        sources = {
            "w0": (W0.rearrange(w_view, t=T), BF16),
            "w1": (W1.rearrange(w_view, t=T), BF16),
            "w2": (W2.rearrange(w_view, t=T), BF16),
            "w3": (W3.rearrange(w_view, t=T), BF16),
            "wc": (Wc.rearrange(w_view, t=T), BF16),
            "q0": (q_view[0], BF16),
            "q1": (q_view[1], BF16),
            "b0": (qh_view[0], U8),
            "b1": (qh_view[1], U8),
        }
        rows = {}
        for load in "b0:0:4 w0:0:2 w0:2:4 q0:0:4 w1:0:4 vec w2:0:4 q1:0:4 b1:0:4 w3:0:4 wc:0:4".split():
            if load == "vec":
                for i, v in enumerate((b0, b1, b2, b3, bc, gG, betaG, gE, betaE)):
                    nc.sync.dma_start(out=vec_bf[:, i, 0:T], in_=v.rearrange("(p t) -> p t", t=T))
                continue
            name, lo, hi = load.split(":")
            view, dt = sources[name]
            if name not in rows:
                rows[name] = raw.tile([P, T, D], dt, name="raw_" + name)
            nc.sync.dma_start(out=rows[name][:, int(lo) : int(hi), :], in_=view[:, int(lo) : int(hi), :])
        for h in range(HALVES):
            rows["x%d" % h] = raw.tile([P, T, D], BF16, name="raw_x%d" % h)

        vec = const.tile([P, 9, T], F32, name="vec")
        nc.gpsimd.tensor_copy(out=vec[:], in_=vec_bf[:, :, 0:T])
        vb0, vb1, vb2, vb3, vbc, vgG, vbG, vgE, vbE = (vec[:, i, :] for i in range(9))
        neg = const.tile([P, 5, T], F32, name="neg")
        nc.gpsimd.tensor_scalar(out=neg[:], in0=vec[:, 0:5, :], scalar1=-1.0, scalar2=0.0, op0=ALU.mult, op1=ALU.add)
        nb0, nb1, nb3, nbc = neg[:, 0, :], neg[:, 1, :], neg[:, 3, :], neg[:, 4, :]
        b01 = const.tile([P, T], F32, name="b01")
        nc.gpsimd.tensor_tensor(out=b01[:], in0=vb0, in1=vb1, op=ALU.add)
        b3c = const.tile([P, T], F32, name="b3c")
        nc.gpsimd.tensor_tensor(out=b3c[:], in0=vb3, in1=vbc, op=ALU.add)
        scale_b = const.tile([P, D], F32, name="scale_b")
        b2_b = const.tile([P, D], F32, name="b2_b")
        s_t = [work.tile([P, T, GN], F32, name="s%d" % g, bufs=1) for g in range(4)]
        y_t = {"0": work.tile([P, T, GN], F32, name="yt0", bufs=1), "1": work.tile([P, T, GN], F32, name="yt1", bufs=1)}
        r3 = [work.tile([P, T, 2 * GN], F32, name="r3%d" % h, bufs=1) for h in range(HALVES)]
        z_t = [[work.tile([P, 2, D], F32, name="z%d%d" % (g, i), bufs=1) for i in range(2)] for g in range(4)]

        st = {}

        def open_bank(shape, idle=True):
            bank = pools[st["pool"]].tile(shape, F32, name="bank")
            flat = bank[:] if len(shape) == 2 else bank[:].rearrange("p a b -> p (a b)" if len(shape) == 3 else "p a b c -> p (a b c)")
            for i in range(st["dum"] if idle else 0):
                nc.tensor.matmul(flat, lhsT=zeros[:, 0:P], rhs=zeros[:], start=True, stop=True)
            return bank

        def copy(eng, out, in_):
            if eng == "S":
                nc.scalar.copy(out=out, in_=in_)
            else:
                nc.vector.tensor_copy(out=out, in_=in_)

        def affine(eng, out, in_, gain, shift):
            if eng == "S":
                nc.scalar.activation(out=out, in_=in_, func=ACT.Identity, bias=shift, scale=gain)
            else:
                nc.vector.tensor_scalar(out=out, in0=in_, scalar1=gain, scalar2=shift, op0=ALU.mult, op1=ALU.add)

        def col(v, t):
            return v[:, int(t) : int(t) + 1]

        def scT():
            st["sc"] = open_bank([P, T, P])
            for t in range(T):
                nc.tensor.transpose(st["sc"][:, t, :], scale_cols[:, t : t + 1].to_broadcast([P, P]), ident[:])

        def scC(eng):
            copy(eng, scale_b[:].rearrange("p (n t) -> p n t", t=T), st["sc"][:].rearrange("p t n -> p n t"))

        def bbT():
            st["bb"] = open_bank([P, T, P])
            for t in range(T):
                nc.tensor.transpose(st["bb"][:, t, :], vb2[:, t : t + 1].to_broadcast([P, P]), ident[:])

        def bbC(eng):
            copy(eng, b2_b[:].rearrange("p (t n) -> p t n", t=T), st["bb"][:])

        def prod(h, j):
            j = int(j)
            nc.vector.tensor_tensor(out=rows["x" + h][:, j, :], in0=rows["b" + h][:, j, :].bitcast(FP8), in1=scale_b[:], op=ALU.mult)

        def uT(name, jj):
            jj = int(jj)
            words = rows[name][:].rearrange("p j k -> p (j k)").bitcast(F32)
            bank = open_bank([P, 2, 2, P])
            for j in range(2):
                for u in range(2):
                    w0 = (2 * jj + j) * 256 + u
                    nc.tensor.transpose(bank[:, j, u, :], words[:, w0 : w0 + 256 - u : 2], ident[:])
            st["b%s%d" % (name, jj)] = bank

        def uC(name, jj, eng):
            jj = int(jj)
            wide = name[0] == "w"
            key = "g" + name + ("" if wide else str(jj))
            if key not in st:
                st[key] = work.tile([P, 2 * D * (2 if wide else 1)], BF16, name="groupw" if wide else "groupx", align_bytes=64, bufs=3)
            gw = st[key][:].bitcast(F32)
            if wide:
                gw = gw[:, 512 * jj : 512 * (jj + 1)]
            copy(eng, gw.rearrange("p (j r u) -> p j r u", j=2, u=2), st["b%s%d" % (name, jj)][:].rearrange("p j u r -> p j r u"))

        def uQ(name, jj=""):
            if "q" + name not in st:
                codes = const.tile([P, 2 * GN], U32, name="codes_" + name, align_bytes=64)
                scales = const.tile([P, 2 * GN], U8, name="scales_" + name, align_bytes=64)
                st["q" + name] = (codes, scales)
            codes, scales = st["q" + name]
            cols = slice(GN * int(jj), GN * int(jj) + GN) if jj else slice(0, 2 * GN)
            nc.vector.quantize_mx(out=codes[:, cols].bitcast(FP8X4), scales=scales[:, cols], in_=st["g" + name + jj][:])

        def mx(dst, w, t, x, toks):
            cols = slice(P * t, P * (t + 1))
            w, x = st[w], st[x]
            nc.tensor.matmul_mx(
                out=dst, lhsT=w[0][:, cols].bitcast(FP8X4), lhsT_scale=w[1][:, cols], rhs=x[0][:, toks].bitcast(FP8X4), rhs_scale=x[1][:, toks], start=True, stop=True
            )

        def aM(g, tt, i):
            bank = open_bank([P, 2, GN], idle=False)
            h, jj = divmod(int(g), 2)
            for n in [0, 1] * (st["dum"] + 1):
                mx(bank[:, n, :], "qw" + i, 2 * int(tt) + n, "q%s%d" % ("q" if i == "0" else "x", h), slice(GN * jj, GN * (jj + 1)))
                st["a%s%d%s" % (g, 2 * int(tt) + n, i)] = bank[:, n, :]

        def rM(h, t):
            bank = open_bank([P, 2 * GN], idle=False)
            for n in range(st["dum"] + 1):
                mx(bank[:], "qw3", int(t), "qq" + h, slice(0, 2 * GN))
            st["R" + h + t] = bank[:]

        def aR(g, t, eng):
            r0 = work.tile([P, GN], F32, name="r0", bufs=6)
            src = st["a" + g + t + "0"]
            if eng == "V":
                nc.vector.tensor_scalar(out=r0[:], in0=src, scalar1=col(nb0, t), scalar2=col(b01, t), op0=ALU.max, op1=ALU.add)
            else:
                nc.scalar.activation(out=r0[:], in_=src, func=ACT.Relu, bias=col(vb0, t), scale=1.0)
                nc.gpsimd.tensor_scalar(out=r0[:], in0=r0[:], scalar1=1.0, scalar2=col(vb1, t), op0=ALU.mult, op1=ALU.add)
            st["r" + g + t] = r0

        def aS(g, t):
            nc.vector.scalar_tensor_tensor(
                out=s_t[int(g)][:, int(t), :], in0=st["a" + g + t + "1"], scalar=col(nb1, t), in1=st["r" + g + t][:], op0=ALU.max, op1=ALU.add
            )

        def aY(g, t, eng):
            dst, src = y_t[g][:, int(t), :], st["a" + g + t + "2"]
            if eng == "S":
                nc.scalar.activation(out=dst, in_=src, func=ACT.Relu, bias=col(vb2, t), scale=1.0)
            else:
                nc.vector.tensor_scalar(out=dst, in0=src, scalar1=col(vb2, t), scalar2=0.0, op0=ALU.add, op1=ALU.max)

        def eM(k):
            bank = open_bank([P, D], idle=False)
            h = int(k) // 4
            x, w = st["qx%d" % h], st["qw2"]
            cols = slice(P * (int(k) % 4), P * (int(k) % 4 + 1))
            for n in range(st["dum"] + 1):
                nc.tensor.matmul_mx(
                    out=bank[:], lhsT=x[0][:, cols].bitcast(FP8X4), lhsT_scale=x[1][:, cols], rhs=w[0][:].bitcast(FP8X4), rhs_scale=w[1][:], start=True, stop=True
                )
            st["E" + k] = bank

        def eU(k):
            y = work.tile([P, D], F32, name="y", bufs=4)
            nc.vector.tensor_tensor(out=y[:], in0=st["E" + k][:], in1=b2_b[:], op=ALU.add)
            st["y" + k] = y

        def eY(k, eng):
            y = st["y" + k]
            engine = nc.vector if eng == "V" else nc.gpsimd
            engine.tensor_scalar(out=y[:], in0=y[:], scalar1=0.0, scalar2=0.0, op0=ALU.max, op1=ALU.add)

        def r3S(h, t, eng):
            dst, src = r3[int(h)][:, int(t), :], st["R" + h + t]
            if eng == "V":
                nc.vector.tensor_scalar(out=dst, in0=src, scalar1=col(nb3, t), scalar2=col(b3c, t), op0=ALU.max, op1=ALU.add)
            else:
                nc.scalar.activation(out=dst, in_=src, func=ACT.Relu, bias=col(vb3, t), scale=1.0)
                nc.gpsimd.tensor_scalar(out=dst, in0=dst, scalar1=1.0, scalar2=col(vbc, t), op0=ALU.mult, op1=ALU.add)

        def bT(k, side):
            g, j = divmod(int(k), 2)
            src = y_t[str(g)] if side == "1" else s_t[g]
            bank = open_bank([P, D])
            for t in range(T):
                nc.tensor.transpose(bank[:, P * t : P * (t + 1)], src[:, t, P * j : P * (j + 1)], ident[:])
            st["B" + k + side] = bank

        def bS(k, side):
            i = int(side)
            if "st" + k not in st:
                st["st" + k] = work.tile([P, 2, 6], F32, name="st", bufs=4)
                st["mv" + k] = work.tile([P, 2, 2], F32, name="mv", bufs=4)
            nc.vector.bn_stats(out=st["st" + k][:, i, :], in_=(st["B" + k + side] if "B" + k + side in st else st["y" + k])[:])

        def bA(k):
            for i in range(2):
                nc.vector.bn_aggr(out=st["mv" + k][:, i, :], in_=st["st" + k][:, i, :])

        def bQ(k):
            rs = work.tile([P, 2], F32, name="rs", bufs=4)
            nc.scalar.activation(out=rs[:], in_=st["mv" + k][:, :, 1], func=ACT.Abs_reciprocal_sqrt, bias=EPS)
            st["rs" + k] = rs

        def bR(k):
            nm = work.tile([P, 2], F32, name="nm", bufs=4)
            for i in range(2):
                if "B%s%d" % (k, i) in st:
                    nc.gpsimd.tensor_scalar(
                        out=nm[:, i : i + 1], in0=st["mv" + k][:, i, 0:1], scalar1=-1.0, scalar2=st["rs" + k][:, i : i + 1], op0=ALU.mult, op1=ALU.mult
                    )
            st["nm" + k] = nm

        def bN(k, side, eng):
            g, j = divmod(int(k), 2)
            z = z_t[g][int(side)][:, j, :]
            if "B" + k + side in st:
                affine(eng, z, st["B" + k + side][:], col(st["rs" + k], side), col(st["nm" + k], side))
            else:
                engine = nc.vector if eng == "V" else nc.gpsimd
                engine.tensor_scalar(out=z, in0=st["y" + k][:], scalar1=st["mv" + k][:, 1, 0:1], scalar2=st["rs" + k][:, 1:2], op0=ALU.subtract, op1=ALU.mult)

        def cT(g, tt, side):
            if "c" + g + side not in st:
                st["c" + g + side] = work.tile([P, T, GN], F32, name="ge"[int(side)])
            bank = open_bank([P, 2, GN])
            for i in range(2):
                t = 2 * int(tt) + i
                for j in range(2):
                    nc.tensor.transpose(bank[:, i, P * j : P * (j + 1)], z_t[int(g)][int(side)][:, j, P * t : P * (t + 1)], ident[:])
                st["C%s%d%s" % (g, t, side)] = bank[:, i, :]

        def cE(g, t, side, eng):
            gain, shift = ((vgG, vbG), (vgE, vbE))[int(side)]
            affine(eng, st["c" + g + side][:, int(t), :], st["C" + g + t + side], col(gain, t), col(shift, t))

        def cM(g, c, eng):
            c = int(c)
            if "cg" + g not in st:
                st["cg" + g] = work.tile([P, 4 * GN], BF16, name="groupge", align_bytes=64)
            toks = slice(P * c, P * (c + 1))
            dst = st["cg" + g][:, 4 * P * c : 4 * P * (c + 1)]
            lhs, rhs = st["c" + g + "0"][:, :, toks], st["c" + g + "1"][:, :, toks]
            if eng == "V":
                split = "p t (n i) -> p n t i"
                nc.vector.tensor_tensor(
                    out=dst.rearrange("p (n i t) -> p n t i", t=T, i=4), in0=lhs.rearrange(split, i=4), in1=rhs.rearrange(split, i=4), op=ALU.mult
                )
            else:
                nc.gpsimd.tensor_tensor(
                    out=dst.rearrange("p (n t) -> p n t", t=T), in0=lhs.rearrange("p t n -> p n t"), in1=rhs.rearrange("p t n -> p n t"), op=ALU.mult
                )

        def cQ(g):
            codes = work.tile([P, GN], U32, name="codes_ge", align_bytes=64)
            scales = work.tile([P, GN], U8, name="scales_ge", align_bytes=64)
            nc.vector.quantize_mx(out=codes[:].bitcast(FP8X4), scales=scales[:], in_=st["cg" + g][:])
            st["qg" + g] = (codes, scales)

        def dM(g, tt):
            bank = open_bank([P, 2, GN], idle=False)
            for i in [0, 1] * (st["dum"] + 1):
                t = 2 * int(tt) + i
                mx(bank[:, i, :], "qwc", t, "qg" + g, slice(0, GN))
                st["D%s%d" % (g, t)] = bank[:, i, :]

        def dS(g, t):
            if "o" + g not in st:
                st["o" + g] = work.tile([P, T, GN], F32, name="o")
            nc.vector.scalar_tensor_tensor(
                out=st["o" + g][:, int(t), :], in0=st["D" + g + t], scalar=col(nbc, t), in1=r3[int(g) // 2][:, int(t), GN * (int(g) % 2) : GN * (int(g) % 2) + GN], op0=ALU.max, op1=ALU.add
            )

        out_v = out[0].rearrange("(h p j) c -> h p j c", h=HALVES, j=T)

        def dT(g, j):
            bank = open_bank([P, T, P])
            for t in range(T):
                nc.tensor.transpose(bank[:, t, :], st["o" + g][:, t, P * int(j) : P * (int(j) + 1)], ident[:])
            st["O" + g + j] = bank

        def dC(g, j, eng):
            h, jp = divmod(int(g), 2)
            fin = work.tile([P, D], F32, name="fin", bufs=4)
            copy(eng, fin[:].rearrange("p (m t) -> p m t", t=T), st["O" + g + j][:].rearrange("p t m -> p m t"))
            nc.sync.dma_start(out=out_v[h, :, 2 * jp + int(j), :], in_=fin[:])

        fns = {
            "scT": scT, "scC": scC, "prod": prod, "uT": uT, "uC": uC, "uQ": uQ, "aM": aM, "aR": aR, "aS": aS, "rM": rM, "aY": aY, "eM": eM, "eU": eU, "eY": eY, "bbT": bbT, "bbC": bbC, "r3S": r3S, "bT": bT, "bS": bS,
            "bA": bA, "bQ": bQ, "bR": bR, "bN": bN, "cT": cT, "cE": cE, "cM": cM, "cQ": cQ, "dM": dM, "dS": dS, "dT": dT, "dC": dC,
        }
        for step in ORDER.split():
            parts = step.split(":")
            word = parts[0].split(".")
            st["pool"], st["dum"] = (parts[1], int(parts[2])) if len(parts) > 1 else ("m", 0)
            fns[word[0]](*word[1:])
